import numpy as np
import ml_dtypes


def mxq(x, axis, fmt="e4m3"):
    dtype, down = {"e4m3": (ml_dtypes.float8_e4m3fn, 7), "e5m2": (ml_dtypes.float8_e5m2, 14)}[fmt]
    v = np.moveaxis(np.asarray(x, np.float32).astype(ml_dtypes.bfloat16).astype(np.float64), axis, -1)
    blocks = v.reshape(v.shape[:-1] + (-1, 32))
    amax = np.abs(blocks).max(-1, keepdims=True)
    byte = np.maximum(np.where(amax > 0, np.frexp(amax)[1] - 1 + 127, 0) - down, 1)
    scale = np.exp2(byte - 127.0)
    codes = (blocks / scale).astype(np.float32).astype(dtype).astype(np.float64)
    return np.moveaxis((codes * scale).reshape(v.shape), -1, axis)


WIDE = False


def mx_kscale(k):
    if not WIDE:
        return np.ones(k)
    levels = np.array([10, -10, 5, -5, 0])
    a = np.random.permutation(np.resize(levels, k // 512 * 4)).reshape(k // 512, 4)
    idx = np.arange(k)
    return np.exp2(a[idx // 512, idx % 128 // 32])


BF16 = ml_dtypes.bfloat16


def bf(x):
    return np.asarray(x, np.float32).astype(BF16)


def f64(x):
    return np.asarray(x).astype(np.float64)


E2M1 = np.array([0.0, 0.5, 1.0, 1.5, 2.0, 3.0, 4.0, 6.0, -0.0, -0.5, -1.0, -1.5, -2.0, -3.0, -4.0, -6.0])


def pack_weight(w, fmt):
    k, n = w.shape
    w = f64(bf(w)).reshape(k // 32, 32, n)
    amax = np.abs(w).max(1)
    if fmt == "e4m3":
        byte = np.frexp(amax)[1] - 1 + 127 - 7
    else:
        mant, ex = np.frexp(amax / 6.0)
        byte = np.where(mant > 0.5, ex, ex - 1) + 127
    byte = np.clip(np.where(amax > 0, byte, 1), 1, 254)
    scaled = (w * np.exp2(127.0 - byte)[:, None, :]).reshape(k, n).astype(np.float32)
    by_word = np.ascontiguousarray(scaled.reshape(k // 512, 128, 4, n).transpose(0, 1, 3, 2))
    if fmt == "e4m3":
        words = by_word.astype(ml_dtypes.float8_e4m3fn).view(np.uint8)
    else:
        c = by_word.astype(ml_dtypes.float4_e2m1fn).view(np.uint8) & 0xF
        words = c[..., 0::2] | (c[..., 1::2] << 4)
    return np.ascontiguousarray(words), np.ascontiguousarray(byte.astype(np.uint8).reshape(k // 512, 16, n))


def unpack_weight(words, scales, fmt):
    g, p, n, _ = words.shape
    if fmt == "e4m3":
        vals = np.ascontiguousarray(words).view(ml_dtypes.float8_e4m3fn).astype(np.float64)
    else:
        nib = np.empty((g, p, n, 4), np.uint8)
        nib[..., 0::2] = words & 0xF
        nib[..., 1::2] = words >> 4
        vals = E2M1[nib]
    vals = vals * np.repeat(np.exp2(scales.astype(np.float64) - 127.0), 8, axis=1)[..., None]
    return vals.transpose(0, 1, 3, 2).reshape(g * 512, n)

def pack4(w):
    words, scales = pack_weight(w, "e2m1")
    return words.reshape(words.shape[0], 128, -1), scales


def unpack4(words, scales):
    return unpack_weight(words.reshape(words.shape[0], 128, -1, 2), scales, "e2m1")


B, I, H = 1024, 512, 512


def sig(v):
    return 1.0 / (1.0 + np.exp(-v))


def setup_inputs():
    s, t = mx_kscale(I), mx_kscale(H)
    x = bf(np.random.standard_normal((B, I)) * s)
    m_prev = bf(np.random.standard_normal((B, H)) * t)
    c_prev = bf(np.random.standard_normal((B, H)))
    w_m_words, w_m_scales = pack4(np.random.standard_normal((H, 8 * H)) / np.sqrt(H) / t[:, None])
    w_inputs_words, w_inputs_scales = pack4(np.random.standard_normal((I, 8 * H)) / np.sqrt(I) / s[:, None])
    return {"x": x,
            "m_prev": m_prev,
            "c_prev": c_prev,
            "w_m_words": w_m_words,
            "w_m_scales": w_m_scales,
            "w_inputs_words": w_inputs_words,
            "w_inputs_scales": w_inputs_scales}


def reference(x, m_prev, c_prev, w_m_words, w_m_scales, w_inputs_words, w_inputs_scales):
    m_mat = mxq(f64(m_prev), 1, "e4m3") @ unpack4(w_m_words, w_m_scales)
    in_mat = mxq(f64(x), 1, "e4m3") @ unpack4(w_inputs_words, w_inputs_scales)
    ms = np.split(m_mat, 8, axis=1)
    xs = np.split(in_mat, 8, axis=1)
    l1_0 = sig(xs[0] + ms[0])
    l1_1 = np.maximum(xs[1] + ms[1], 0.0)
    l1_2 = sig(xs[2] + ms[2])
    l1_3 = np.maximum(xs[3] * ms[3], 0.0)
    l1_4 = np.tanh(xs[4] + ms[4])
    l1_5 = sig(xs[5] + ms[5])
    l1_6 = np.tanh(xs[6] + ms[6])
    l1_7 = sig(xs[7] + ms[7])
    l2_0 = np.tanh(l1_0 * l1_1)
    l2_1 = np.tanh(l1_2 + l1_3)
    l2_2 = np.tanh(l1_4 * l1_5)
    l2_3 = sig(l1_6 + l1_7)
    l2_0 = np.tanh(l2_0 + f64(c_prev))
    new_c = l2_0 * l2_1
    l3_1 = np.tanh(l2_2 + l2_3)
    new_m = np.tanh(new_c * l3_1)
    return (new_m, new_c)

@@ -1,0 +1,198 @@
+import concourse.mybir as mybir
+from concourse.masks import make_identity
+
+F32 = mybir.dt.float32
+BF16 = mybir.dt.bfloat16
+I32 = mybir.dt.int32
+U8 = mybir.dt.uint8
+U32 = mybir.dt.uint32
+FP8X4 = mybir.dt.float8_e4m3fn_x4
+FP4X4 = mybir.dt.float4_e2m1fn_x4
+ACT = mybir.ActivationFunctionType
+ALU = mybir.AluOpType
+
+P = 128
+B = 1024
+K = 512
+H = 512
+GATES = 8
+TILES = B // P
+FLOPS = 2 * 2 * B * K * GATES * H
+
+
+def tile_nascell_kernel(tc, x, m_prev, c_prev, w_m_words, w_m_scales, w_inputs_words, w_inputs_scales, out_0, out_1):
+    nc = tc.nc
+    act_d = (x.rearrange("(p i) k -> p i k", i=TILES), m_prev.rearrange("(p i) k -> p i k", i=TILES))
+    c_v = c_prev.rearrange("(p i) k -> p i k", i=TILES)
+    new_m_v = out_0.rearrange("(p i) h -> p i h", i=TILES)
+    new_c_v = out_1.rearrange("(p i) h -> p i h", i=TILES)
+    words_d = (w_inputs_words.flatten_outer_dims(), w_m_words.flatten_outer_dims())
+    scales_d = (w_inputs_scales.flatten_outer_dims(), w_m_scales.flatten_outer_dims())
+
+    with tc.tile_pool(name="keep", bufs=1) as keep, tc.tile_pool(name="work", bufs=3) as work, tc.psum_pool(name="psum", bufs=8) as psum, tc.manual_schedule():
+        ident = keep.tile([P, P], F32)
+        warm = keep.tile([P, 1], F32)
+        act_sb = keep.tile([P, 2, TILES, K], BF16)
+        c_sb = keep.tile([P, TILES, H], BF16)
+        w_x = keep.tile([P, 2 * GATES * H], U8, align_bytes=64)
+        w_m = keep.tile([P, 2 * GATES * H], U8, align_bytes=64)
+        s_x = keep.tile([P, GATES * H], U8, align_bytes=64)
+        s_m = keep.tile([P, GATES * H], U8, align_bytes=64)
+        grouped = keep.tile([P, TILES, 2, 4 * P], BF16, align_bytes=64)
+        codes = keep.tile([P, TILES, 2, P], U32, align_bytes=64)
+        a_scales = keep.tile([P, TILES, 2, P], U8, align_bytes=64)
+        w_sb = (w_x, w_m)
+        s_sb = (s_x, s_m)
+
+        nc.vector.memset(s_x[:].bitcast(I32), 0)
+        nc.vector.memset(s_m[:].bitcast(I32), 0)
+        nc.vector.memset(warm[:], 0.0)
+        nc.scalar.activation(out=warm[:], in_=warm[:], func=ACT.Sigmoid)
+        make_identity(nc, ident[:])
+
+        def load_rows(o, lo, hi):
+            nc.sync.dma_start(out=act_sb[:, o, lo:hi, :], in_=act_d[o][:, lo:hi, :])
+
+        def load_words(o, pair):
+            cols = slice(pair * 4 * H, (pair + 1) * 4 * H)
+            nc.sync.dma_start(out=w_sb[o][:, cols].bitcast(I32), in_=words_d[o][:, cols].bitcast(I32))
+
+        def load_scales(o):
+            for r in range(4):
+                nc.sync.dma_start(out=s_sb[o][r:P:32, :].bitcast(I32), in_=scales_d[o][r:16:4, :].bitcast(I32))
+
+        load_rows(0, 0, 1)
+        load_rows(1, 0, 1)
+        load_scales(0)
+        load_words(0, 2)
+        load_words(1, 2)
+        load_scales(1)
+        load_words(0, 3)
+        load_words(1, 3)
+        load_rows(0, 1, 2)
+        load_rows(1, 1, 2)
+        load_words(0, 0)
+        load_words(1, 0)
+        load_words(0, 1)
+        load_words(1, 1)
+        nc.sync.dma_start(out=c_sb[:, 0:2, :], in_=c_v[:, 0:2, :])
+        load_rows(0, 2, 4)
+        load_rows(1, 2, 4)
+        load_rows(0, 4, 8)
+        load_rows(1, 4, 8)
+        nc.sync.dma_start(out=c_sb[:, 2:TILES, :], in_=c_v[:, 2:TILES, :])
+
+        live = {}
+
+        def there(i):
+            return 0 <= i < TILES
+
+        def flip(i):
+            if there(i):
+                flipped = psum.tile([P, 2, 2, P], F32, tag="bank")
+                for o in range(2):
+                    as_words = act_sb[:, o, i, :].bitcast(F32)
+                    for u in range(2):
+                        nc.tensor.transpose(flipped[:, o, u, :], as_words[:, u:K // 2:2], ident[:])
+                live[("flipped", i)] = flipped
+
+        def regroup(i):
+            if there(i):
+                nc.vector.tensor_copy(
+                    out=grouped[:, i].bitcast(F32).rearrange("p o (r u) -> p o r u", u=2),
+                    in_=live[("flipped", i)][:].rearrange("p o u r -> p o r u"),
+                )
+
+        def quantise(i):
+            if there(i):
+                nc.vector.quantize_mx(
+                    out=codes[:, i].rearrange("p o r -> p (o r)").bitcast(FP8X4),
+                    scales=a_scales[:, i].rearrange("p o r -> p (o r)"),
+                    in_=grouped[:, i].rearrange("p o c -> p (o c)"),
+                )
+
+        def product(name, i, g, operands):
+            if there(i):
+                bank = psum.tile([P, H], F32, tag="bank", name=name)
+                for o in operands:
+                    nc.tensor.matmul_mx(
+                        out=bank[:],
+                        lhsT=codes[:, i, o, :].bitcast(FP8X4),
+                        lhsT_scale=a_scales[:, i, o, :],
+                        rhs=w_sb[o][:, g * 2 * H:(g + 1) * 2 * H].bitcast(FP4X4),
+                        rhs_scale=s_sb[o][:, g * H:(g + 1) * H],
+                        start=(o == operands[0]),
+                        stop=(o == operands[-1]),
+                    )
+                live[(name, i)] = bank[:]
+
+        def fresh(name, i):
+            made = work.tile([P, H], F32, tag=name, name=name)
+            live[(name, i)] = made[:]
+            return made[:]
+
+        def scalar(name, func, src, i):
+            if there(i):
+                nc.scalar.activation(out=fresh(name, i), in_=live[(src, i)], func=func)
+
+        def vector(name, a, op, b, i):
+            if there(i):
+                nc.vector.tensor_tensor(out=fresh(name, i), in0=live[(a, i)], in1=live[(b, i)], op=op)
+
+        def vector_relu(name, a, op, b, i):
+            if there(i):
+                nc.vector.scalar_tensor_tensor(out=fresh(name, i), in0=live[(a, i)], scalar=0.0, in1=live[(b, i)], op0=ALU.max, op1=op)
+
+        def vector_copy(name, a, i):
+            if there(i):
+                nc.vector.tensor_copy(out=fresh(name, i), in_=live[(a, i)])
+
+        def store(dram, name, i):
+            if there(i):
+                nc.sync.dma_start(out=dram[:, i, :], in_=live[(name, i)])
+
+        for i in range(TILES):
+            live[("c", i)] = c_sb[:, i, :]
+
+        flip(0)
+        regroup(0)
+        quantise(0)
+        for p in range(TILES + 2):
+            product("s4", p, 4, (0, 1))
+            product("s5", p, 5, (0, 1))
+            product("s6", p, 6, (0, 1))
+            product("s7", p, 7, (0, 1))
+            flip(p + 1)
+            product("s0", p, 0, (0, 1))
+            product("s1", p, 1, (0, 1))
+            product("s2", p, 2, (0, 1))
+            product("x3", p, 3, (0,))
+            product("m3", p, 3, (1,))
+
+            vector_relu("z1", "p3", ALU.add, "a2", p - 1)
+            scalar("a4", ACT.Tanh, "s4", p)
+            scalar("u0", ACT.Tanh, "z0", p - 1)
+            vector("z5", "b2", ALU.add, "b3", p - 1)
+            scalar("a5", ACT.Sigmoid, "s5", p)
+            vector("z6", "new_c", ALU.mult, "l3", p - 2)
+            scalar("b1", ACT.Tanh, "z1", p - 1)
+            vector("v0", "u0", ALU.add, "c", p - 1)
+            scalar("a6", ACT.Tanh, "s6", p)
+            vector("z2", "a4", ALU.mult, "a5", p)
+            scalar("new_m", ACT.Tanh, "z6", p - 2)
+            store(new_m_v, "new_m", p - 2)
+            regroup(p + 1)
+            scalar("a7", ACT.Sigmoid, "s7", p)
+            quantise(p + 1)
+            scalar("b0", ACT.Tanh, "v0", p - 1)
+            vector("z3", "a6", ALU.add, "a7", p)
+            scalar("a0", ACT.Sigmoid, "s0", p)
+            vector("new_c", "b0", ALU.mult, "b1", p - 1)
+            store(new_c_v, "new_c", p - 1)
+            scalar("b2", ACT.Tanh, "z2", p)
+            vector_relu("z0", "s1", ALU.mult, "a0", p)
+            scalar("a2", ACT.Sigmoid, "s2", p)
+            vector_copy("c3", "x3", p)
+            scalar("b3", ACT.Sigmoid, "z3", p)
+            vector("p3", "m3", ALU.mult, "c3", p)
+            scalar("l3", ACT.Tanh, "z5", p - 1)

@@ -18,6 +18,8 @@ H = 512
 GATES = 8
 TILES = B // P
 FLOPS = 2 * 2 * B * K * GATES * H
+WHOLE = (slice(0, H),)
+HALVES = (slice(0, H // 2), slice(H // 2, H))
 
 
 def tile_nascell_kernel(tc, x, m_prev, c_prev, w_m_words, w_m_scales, w_inputs_words, w_inputs_scales, out_0, out_1):
@@ -32,6 +34,7 @@ def tile_nascell_kernel(tc, x, m_prev, c_prev, w_m_words, w_m_scales, w_inputs_w
     with tc.tile_pool(name="keep", bufs=1) as keep, tc.tile_pool(name="work", bufs=3) as work, tc.psum_pool(name="psum", bufs=8) as psum, tc.manual_schedule():
         ident = keep.tile([P, P], F32)
         warm = keep.tile([P, 1], F32)
+        zeros = keep.tile([P, H], BF16)
         act_sb = keep.tile([P, 2, TILES, K], BF16)
         c_sb = keep.tile([P, TILES, H], BF16)
         w_x = keep.tile([P, 2 * GATES * H], U8, align_bytes=64)
@@ -44,6 +47,7 @@ def tile_nascell_kernel(tc, x, m_prev, c_prev, w_m_words, w_m_scales, w_inputs_w
         w_sb = (w_x, w_m)
         s_sb = (s_x, s_m)
 
+        nc.vector.memset(zeros[:], 0.0)
         nc.vector.memset(s_x[:].bitcast(I32), 0)
         nc.vector.memset(s_m[:].bitcast(I32), 0)
         nc.vector.memset(warm[:], 0.0)
@@ -87,28 +91,35 @@ def tile_nascell_kernel(tc, x, m_prev, c_prev, w_m_words, w_m_scales, w_inputs_w
         def there(i):
             return 0 <= i < TILES
 
-        def flip(i):
+        def cuts(p):
+            return WHOLE if p < TILES else HALVES
+
+        def spin(turns):
+            for turn in range(turns):
+                nc.tensor.matmul(out=live["idle"][:], lhsT=zeros[:, 0:P], rhs=zeros[:], start=True, stop=True)
+
+        def flip(i, lo, hi):
             if there(i):
-                flipped = psum.tile([P, 2, 2, P], F32, tag="bank")
-                for o in range(2):
+                flipped = psum.tile([P, hi - lo, 2, P], F32, tag="bank")
+                for o in range(lo, hi):
                     as_words = act_sb[:, o, i, :].bitcast(F32)
                     for u in range(2):
-                        nc.tensor.transpose(flipped[:, o, u, :], as_words[:, u:K // 2:2], ident[:])
-                live[("flipped", i)] = flipped
+                        nc.tensor.transpose(flipped[:, o - lo, u, :], as_words[:, u:K // 2:2], ident[:])
+                live[("flipped", i, lo)] = flipped
 
-        def regroup(i):
+        def regroup(i, lo, hi):
             if there(i):
                 nc.vector.tensor_copy(
-                    out=grouped[:, i].bitcast(F32).rearrange("p o (r u) -> p o r u", u=2),
-                    in_=live[("flipped", i)][:].rearrange("p o u r -> p o r u"),
+                    out=grouped[:, i, lo:hi].bitcast(F32).rearrange("p o (r u) -> p o r u", u=2),
+                    in_=live[("flipped", i, lo)][:].rearrange("p o u r -> p o r u"),
                 )
 
-        def quantise(i):
+        def quantise(i, lo, hi):
             if there(i):
                 nc.vector.quantize_mx(
-                    out=codes[:, i].rearrange("p o r -> p (o r)").bitcast(FP8X4),
-                    scales=a_scales[:, i].rearrange("p o r -> p (o r)"),
-                    in_=grouped[:, i].rearrange("p o c -> p (o c)"),
+                    out=codes[:, i, lo:hi].rearrange("p o r -> p (o r)").bitcast(FP8X4),
+                    scales=a_scales[:, i, lo:hi].rearrange("p o r -> p (o r)"),
+                    in_=grouped[:, i, lo:hi].rearrange("p o c -> p (o c)"),
                 )
 
         def product(name, i, g, operands):
@@ -131,68 +142,86 @@ def tile_nascell_kernel(tc, x, m_prev, c_prev, w_m_words, w_m_scales, w_inputs_w
             live[(name, i)] = made[:]
             return made[:]
 
-        def scalar(name, func, src, i):
+        def scalar(name, func, src, p, lag):
+            i = p - lag
             if there(i):
-                nc.scalar.activation(out=fresh(name, i), in_=live[(src, i)], func=func)
+                out = fresh(name, i)
+                for cols in cuts(p):
+                    nc.scalar.activation(out=out[:, cols], in_=live[(src, i)][:, cols], func=func)
 
-        def vector(name, a, op, b, i):
+        def vector(name, a, op, b, p, lag):
+            i = p - lag
             if there(i):
-                nc.vector.tensor_tensor(out=fresh(name, i), in0=live[(a, i)], in1=live[(b, i)], op=op)
+                out = fresh(name, i)
+                for cols in cuts(p):
+                    nc.vector.tensor_tensor(out=out[:, cols], in0=live[(a, i)][:, cols], in1=live[(b, i)][:, cols], op=op)
 
-        def vector_relu(name, a, op, b, i):
+        def vector_relu(name, a, op, b, p, lag):
+            i = p - lag
             if there(i):
-                nc.vector.scalar_tensor_tensor(out=fresh(name, i), in0=live[(a, i)], scalar=0.0, in1=live[(b, i)], op0=ALU.max, op1=op)
+                out = fresh(name, i)
+                for cols in cuts(p):
+                    nc.vector.scalar_tensor_tensor(out=out[:, cols], in0=live[(a, i)][:, cols], scalar=0.0, in1=live[(b, i)][:, cols], op0=ALU.max, op1=op)
 
-        def vector_copy(name, a, i):
+        def vector_copy(name, a, p, lag):
+            i = p - lag
             if there(i):
                 nc.vector.tensor_copy(out=fresh(name, i), in_=live[(a, i)])
 
-        def store(dram, name, i):
+        def store(dram, name, p, lag):
+            i = p - lag
             if there(i):
-                nc.sync.dma_start(out=dram[:, i, :], in_=live[(name, i)])
+                for cols in cuts(p):
+                    nc.sync.dma_start(out=dram[:, i, cols], in_=live[(name, i)][:, cols])
 
         for i in range(TILES):
             live[("c", i)] = c_sb[:, i, :]
 
-        flip(0)
-        regroup(0)
-        quantise(0)
+        live["idle"] = psum.tile([P, H], F32, tag="bank", name="idle")
+        spin(5)
+        flip(0, 0, 1)
+        flip(0, 1, 2)
+        spin(3)
+        regroup(0, 0, 1)
+        regroup(0, 1, 2)
+        quantise(0, 0, 1)
+        quantise(0, 1, 2)
         for p in range(TILES + 2):
             product("s4", p, 4, (0, 1))
             product("s5", p, 5, (0, 1))
             product("s6", p, 6, (0, 1))
             product("s7", p, 7, (0, 1))
-            flip(p + 1)
+            flip(p + 1, 0, 2)
             product("s0", p, 0, (0, 1))
             product("s1", p, 1, (0, 1))
             product("s2", p, 2, (0, 1))
             product("x3", p, 3, (0,))
             product("m3", p, 3, (1,))
 
-            vector_relu("z1", "p3", ALU.add, "a2", p - 1)
-            scalar("a4", ACT.Tanh, "s4", p)
-            scalar("u0", ACT.Tanh, "z0", p - 1)
-            vector("z5", "b2", ALU.add, "b3", p - 1)
-            scalar("a5", ACT.Sigmoid, "s5", p)
-            vector("z6", "new_c", ALU.mult, "l3", p - 2)
-            scalar("b1", ACT.Tanh, "z1", p - 1)
-            vector("v0", "u0", ALU.add, "c", p - 1)
-            scalar("a6", ACT.Tanh, "s6", p)
-            vector("z2", "a4", ALU.mult, "a5", p)
-            scalar("new_m", ACT.Tanh, "z6", p - 2)
-            store(new_m_v, "new_m", p - 2)
-            regroup(p + 1)
-            scalar("a7", ACT.Sigmoid, "s7", p)
-            quantise(p + 1)
-            scalar("b0", ACT.Tanh, "v0", p - 1)
-            vector("z3", "a6", ALU.add, "a7", p)
-            scalar("a0", ACT.Sigmoid, "s0", p)
-            vector("new_c", "b0", ALU.mult, "b1", p - 1)
-            store(new_c_v, "new_c", p - 1)
-            scalar("b2", ACT.Tanh, "z2", p)
-            vector_relu("z0", "s1", ALU.mult, "a0", p)
-            scalar("a2", ACT.Sigmoid, "s2", p)
-            vector_copy("c3", "x3", p)
-            scalar("b3", ACT.Sigmoid, "z3", p)
-            vector("p3", "m3", ALU.mult, "c3", p)
-            scalar("l3", ACT.Tanh, "z5", p - 1)
+            vector_relu("z1", "p3", ALU.add, "a2", p, 1)
+            scalar("a4", ACT.Tanh, "s4", p, 0)
+            scalar("u0", ACT.Tanh, "z0", p, 1)
+            vector("z6", "new_c", ALU.mult, "l3", p, 2)
+            scalar("a5", ACT.Sigmoid, "s5", p, 0)
+            vector("v0", "u0", ALU.add, "c", p, 1)
+            scalar("b1", ACT.Tanh, "z1", p, 1)
+            vector("z5", "b2", ALU.add, "b3", p, 1)
+            scalar("a6", ACT.Tanh, "s6", p, 0)
+            vector("z2", "a4", ALU.mult, "a5", p, 0)
+            scalar("new_m", ACT.Tanh, "z6", p, 2)
+            store(new_m_v, "new_m", p, 2)
+            regroup(p + 1, 0, 2)
+            scalar("a7", ACT.Sigmoid, "s7", p, 0)
+            quantise(p + 1, 0, 2)
+            scalar("b0", ACT.Tanh, "v0", p, 1)
+            vector("z3", "a6", ALU.add, "a7", p, 0)
+            scalar("a0", ACT.Sigmoid, "s0", p, 0)
+            vector("new_c", "b0", ALU.mult, "b1", p, 1)
+            store(new_c_v, "new_c", p, 1)
+            scalar("b2", ACT.Tanh, "z2", p, 0)
+            vector_relu("z0", "s1", ALU.mult, "a0", p, 0)
+            scalar("a2", ACT.Sigmoid, "s2", p, 0)
+            vector_copy("c3", "x3", p, 0)
+            scalar("b3", ACT.Sigmoid, "z3", p, 0)
+            vector("p3", "m3", ALU.mult, "c3", p, 0)
+            scalar("l3", ACT.Tanh, "z5", p, 1)

@@ -34,7 +34,6 @@ def tile_nascell_kernel(tc, x, m_prev, c_prev, w_m_words, w_m_scales, w_inputs_w
     with tc.tile_pool(name="keep", bufs=1) as keep, tc.tile_pool(name="work", bufs=3) as work, tc.psum_pool(name="psum", bufs=8) as psum, tc.manual_schedule():
         ident = keep.tile([P, P], F32)
         warm = keep.tile([P, 1], F32)
-        zeros = keep.tile([P, H], BF16)
         act_sb = keep.tile([P, 2, TILES, K], BF16)
         c_sb = keep.tile([P, TILES, H], BF16)
         w_x = keep.tile([P, 2 * GATES * H], U8, align_bytes=64)
@@ -47,7 +46,6 @@ def tile_nascell_kernel(tc, x, m_prev, c_prev, w_m_words, w_m_scales, w_inputs_w
         w_sb = (w_x, w_m)
         s_sb = (s_x, s_m)
 
-        nc.vector.memset(zeros[:], 0.0)
         nc.vector.memset(s_x[:].bitcast(I32), 0)
         nc.vector.memset(s_m[:].bitcast(I32), 0)
         nc.vector.memset(warm[:], 0.0)
@@ -93,10 +91,6 @@ def tile_nascell_kernel(tc, x, m_prev, c_prev, w_m_words, w_m_scales, w_inputs_w
 
         def cuts(p):
             return WHOLE if p < TILES else HALVES
-
-        def spin(turns):
-            for turn in range(turns):
-                nc.tensor.matmul(out=live["idle"][:], lhsT=zeros[:, 0:P], rhs=zeros[:], start=True, stop=True)
 
         def flip(i, lo, hi):
             if there(i):
@@ -177,11 +171,8 @@ def tile_nascell_kernel(tc, x, m_prev, c_prev, w_m_words, w_m_scales, w_inputs_w
         for i in range(TILES):
             live[("c", i)] = c_sb[:, i, :]
 
-        live["idle"] = psum.tile([P, H], F32, tag="bank", name="idle")
-        spin(5)
         flip(0, 0, 1)
         flip(0, 1, 2)
-        spin(3)
         regroup(0, 0, 1)
         regroup(0, 1, 2)
         quantise(0, 0, 1)

@@ -55,8 +55,8 @@ def tile_nascell_kernel(tc, x, m_prev, c_prev, w_m_words, w_m_scales, w_inputs_w
         def load_rows(o, lo, hi):
             nc.sync.dma_start(out=act_sb[:, o, lo:hi, :], in_=act_d[o][:, lo:hi, :])
 
-        def load_words(o, pair):
-            cols = slice(pair * 4 * H, (pair + 1) * 4 * H)
+        def load_words(o, first, last):
+            cols = slice(first * 2 * H, (last + 1) * 2 * H)
             nc.sync.dma_start(out=w_sb[o][:, cols].bitcast(I32), in_=words_d[o][:, cols].bitcast(I32))
 
         def load_scales(o):
@@ -66,17 +66,19 @@ def tile_nascell_kernel(tc, x, m_prev, c_prev, w_m_words, w_m_scales, w_inputs_w
         load_rows(0, 0, 1)
         load_rows(1, 0, 1)
         load_scales(0)
-        load_words(0, 2)
-        load_words(1, 2)
         load_scales(1)
-        load_words(0, 3)
-        load_words(1, 3)
+        load_words(0, 4, 4)
+        load_words(1, 4, 4)
+        load_words(0, 5, 5)
+        load_words(1, 5, 5)
+        load_words(0, 6, 7)
+        load_words(1, 6, 7)
         load_rows(0, 1, 2)
         load_rows(1, 1, 2)
-        load_words(0, 0)
-        load_words(1, 0)
-        load_words(0, 1)
-        load_words(1, 1)
+        load_words(0, 0, 1)
+        load_words(1, 0, 1)
+        load_words(0, 2, 3)
+        load_words(1, 2, 3)
         nc.sync.dma_start(out=c_sb[:, 0:2, :], in_=c_v[:, 0:2, :])
         load_rows(0, 2, 4)
         load_rows(1, 2, 4)

@@ -92,7 +92,7 @@ def tile_nascell_kernel(tc, x, m_prev, c_prev, w_m_words, w_m_scales, w_inputs_w
             return 0 <= i < TILES
 
         def cuts(p):
-            return WHOLE if p < TILES else HALVES
+            return WHOLE
 
         def flip(i, lo, hi):
             if there(i):
@@ -173,12 +173,9 @@ def tile_nascell_kernel(tc, x, m_prev, c_prev, w_m_words, w_m_scales, w_inputs_w
         for i in range(TILES):
             live[("c", i)] = c_sb[:, i, :]
 
-        flip(0, 0, 1)
-        flip(0, 1, 2)
-        regroup(0, 0, 1)
-        regroup(0, 1, 2)
-        quantise(0, 0, 1)
-        quantise(0, 1, 2)
+        flip(0, 0, 2)
+        regroup(0, 0, 2)
+        quantise(0, 0, 2)
         for p in range(TILES + 2):
             product("s4", p, 4, (0, 1))
             product("s5", p, 5, (0, 1))

@@ -92,7 +92,7 @@ def tile_nascell_kernel(tc, x, m_prev, c_prev, w_m_words, w_m_scales, w_inputs_w
             return 0 <= i < TILES
 
         def cuts(p):
-            return WHOLE
+            return WHOLE if p < TILES else HALVES
 
         def flip(i, lo, hi):
             if there(i):
@@ -173,9 +173,12 @@ def tile_nascell_kernel(tc, x, m_prev, c_prev, w_m_words, w_m_scales, w_inputs_w
         for i in range(TILES):
             live[("c", i)] = c_sb[:, i, :]
 
-        flip(0, 0, 2)
-        regroup(0, 0, 2)
-        quantise(0, 0, 2)
+        flip(0, 0, 1)
+        flip(0, 1, 2)
+        regroup(0, 0, 1)
+        regroup(0, 1, 2)
+        quantise(0, 0, 1)
+        quantise(0, 1, 2)
         for p in range(TILES + 2):
             product("s4", p, 4, (0, 1))
             product("s5", p, 5, (0, 1))
@@ -191,27 +194,27 @@ def tile_nascell_kernel(tc, x, m_prev, c_prev, w_m_words, w_m_scales, w_inputs_w
             vector_relu("z1", "p3", ALU.add, "a2", p, 1)
             scalar("a4", ACT.Tanh, "s4", p, 0)
             scalar("u0", ACT.Tanh, "z0", p, 1)
-            vector("z6", "new_c", ALU.mult, "l3", p, 2)
             scalar("a5", ACT.Sigmoid, "s5", p, 0)
             vector("v0", "u0", ALU.add, "c", p, 1)
             scalar("b1", ACT.Tanh, "z1", p, 1)
             vector("z5", "b2", ALU.add, "b3", p, 1)
             scalar("a6", ACT.Tanh, "s6", p, 0)
             vector("z2", "a4", ALU.mult, "a5", p, 0)
-            scalar("new_m", ACT.Tanh, "z6", p, 2)
-            store(new_m_v, "new_m", p, 2)
-            regroup(p + 1, 0, 2)
-            scalar("a7", ACT.Sigmoid, "s7", p, 0)
-            quantise(p + 1, 0, 2)
             scalar("b0", ACT.Tanh, "v0", p, 1)
-            vector("z3", "a6", ALU.add, "a7", p, 0)
-            scalar("a0", ACT.Sigmoid, "s0", p, 0)
+            regroup(p + 1, 0, 2)
+            quantise(p + 1, 0, 2)
+            scalar("a7", ACT.Sigmoid, "s7", p, 0)
             vector("new_c", "b0", ALU.mult, "b1", p, 1)
             store(new_c_v, "new_c", p, 1)
+            scalar("l3", ACT.Tanh, "z5", p, 1)
+            vector("z3", "a6", ALU.add, "a7", p, 0)
+            scalar("a0", ACT.Sigmoid, "s0", p, 0)
+            vector("z6", "new_c", ALU.mult, "l3", p, 1)
             scalar("b2", ACT.Tanh, "z2", p, 0)
             vector_relu("z0", "s1", ALU.mult, "a0", p, 0)
             scalar("a2", ACT.Sigmoid, "s2", p, 0)
             vector_copy("c3", "x3", p, 0)
             scalar("b3", ACT.Sigmoid, "z3", p, 0)
             vector("p3", "m3", ALU.mult, "c3", p, 0)
-            scalar("l3", ACT.Tanh, "z5", p, 1)
+            scalar("new_m", ACT.Tanh, "z6", p, 2)
+            store(new_m_v, "new_m", p, 2)

@@ -191,30 +191,30 @@ def tile_nascell_kernel(tc, x, m_prev, c_prev, w_m_words, w_m_scales, w_inputs_w
             product("x3", p, 3, (0,))
             product("m3", p, 3, (1,))
 
+            vector("z5", "b2", ALU.add, "b3", p, 1)
             vector_relu("z1", "p3", ALU.add, "a2", p, 1)
             scalar("a4", ACT.Tanh, "s4", p, 0)
             scalar("u0", ACT.Tanh, "z0", p, 1)
-            scalar("a5", ACT.Sigmoid, "s5", p, 0)
             vector("v0", "u0", ALU.add, "c", p, 1)
-            scalar("b1", ACT.Tanh, "z1", p, 1)
-            vector("z5", "b2", ALU.add, "b3", p, 1)
-            scalar("a6", ACT.Tanh, "s6", p, 0)
+            scalar("a5", ACT.Sigmoid, "s5", p, 0)
             vector("z2", "a4", ALU.mult, "a5", p, 0)
-            scalar("b0", ACT.Tanh, "v0", p, 1)
+            scalar("b1", ACT.Tanh, "z1", p, 1)
             regroup(p + 1, 0, 2)
-            quantise(p + 1, 0, 2)
-            scalar("a7", ACT.Sigmoid, "s7", p, 0)
+            scalar("b0", ACT.Tanh, "v0", p, 1)
             vector("new_c", "b0", ALU.mult, "b1", p, 1)
             store(new_c_v, "new_c", p, 1)
-            scalar("l3", ACT.Tanh, "z5", p, 1)
+            quantise(p + 1, 0, 2)
+            scalar("a6", ACT.Tanh, "s6", p, 0)
+            scalar("a7", ACT.Sigmoid, "s7", p, 0)
             vector("z3", "a6", ALU.add, "a7", p, 0)
-            scalar("a0", ACT.Sigmoid, "s0", p, 0)
+            scalar("l3", ACT.Tanh, "z5", p, 1)
+            vector_copy("c3", "x3", p, 0)
             vector("z6", "new_c", ALU.mult, "l3", p, 1)
             scalar("b2", ACT.Tanh, "z2", p, 0)
-            vector_relu("z0", "s1", ALU.mult, "a0", p, 0)
-            scalar("a2", ACT.Sigmoid, "s2", p, 0)
-            vector_copy("c3", "x3", p, 0)
-            scalar("b3", ACT.Sigmoid, "z3", p, 0)
+            scalar("a0", ACT.Sigmoid, "s0", p, 0)
             vector("p3", "m3", ALU.mult, "c3", p, 0)
+            vector_relu("z0", "s1", ALU.mult, "a0", p, 0)
+            scalar("b3", ACT.Sigmoid, "z3", p, 0)
+            scalar("a2", ACT.Sigmoid, "s2", p, 0)
             scalar("new_m", ACT.Tanh, "z6", p, 2)
             store(new_m_v, "new_m", p, 2)

@@ -34,6 +34,7 @@ def tile_nascell_kernel(tc, x, m_prev, c_prev, w_m_words, w_m_scales, w_inputs_w
     with tc.tile_pool(name="keep", bufs=1) as keep, tc.tile_pool(name="work", bufs=3) as work, tc.psum_pool(name="psum", bufs=8) as psum, tc.manual_schedule():
         ident = keep.tile([P, P], F32)
         warm = keep.tile([P, 1], F32)
+        heat = keep.tile([P, H], BF16)
         act_sb = keep.tile([P, 2, TILES, K], BF16)
         c_sb = keep.tile([P, TILES, H], BF16)
         w_x = keep.tile([P, 2 * GATES * H], U8, align_bytes=64)
@@ -46,6 +47,7 @@ def tile_nascell_kernel(tc, x, m_prev, c_prev, w_m_words, w_m_scales, w_inputs_w
         w_sb = (w_x, w_m)
         s_sb = (s_x, s_m)
 
+        nc.gpsimd.memset(heat[:], 0.0)
         nc.vector.memset(s_x[:].bitcast(I32), 0)
         nc.vector.memset(s_m[:].bitcast(I32), 0)
         nc.vector.memset(warm[:], 0.0)
@@ -65,10 +67,10 @@ def tile_nascell_kernel(tc, x, m_prev, c_prev, w_m_words, w_m_scales, w_inputs_w
 
         load_rows(0, 0, 1)
         load_rows(1, 0, 1)
-        load_scales(0)
-        load_scales(1)
         load_words(0, 4, 4)
         load_words(1, 4, 4)
+        load_scales(0)
+        load_scales(1)
         load_words(0, 5, 5)
         load_words(1, 5, 5)
         load_words(0, 6, 7)
@@ -173,8 +175,15 @@ def tile_nascell_kernel(tc, x, m_prev, c_prev, w_m_words, w_m_scales, w_inputs_w
         for i in range(TILES):
             live[("c", i)] = c_sb[:, i, :]
 
+        def heat_tensor(count):
+            unread = psum.tile([P, H], F32, tag="bank", name="unread")
+            for n in range(count):
+                nc.tensor.matmul(out=unread[:], lhsT=heat[:, 0:P], rhs=heat[:], start=True, stop=True)
+
+        heat_tensor(5)
         flip(0, 0, 1)
         flip(0, 1, 2)
+        heat_tensor(2)
         regroup(0, 0, 1)
         regroup(0, 1, 2)
         quantise(0, 0, 1)

@@ -212,17 +212,20 @@ def tile_nascell_kernel(tc, x, m_prev, c_prev, w_m_words, w_m_scales, w_inputs_w
             scalar("b0", ACT.Tanh, "v0", p, 1)
             vector("new_c", "b0", ALU.mult, "b1", p, 1)
             store(new_c_v, "new_c", p, 1)
-            quantise(p + 1, 0, 2)
+            if p > 0:
+                quantise(p + 1, 0, 2)
             scalar("a6", ACT.Tanh, "s6", p, 0)
             scalar("a7", ACT.Sigmoid, "s7", p, 0)
             vector("z3", "a6", ALU.add, "a7", p, 0)
+            if p == 0:
+                quantise(p + 1, 0, 2)
             scalar("l3", ACT.Tanh, "z5", p, 1)
             vector_copy("c3", "x3", p, 0)
             vector("z6", "new_c", ALU.mult, "l3", p, 1)
             scalar("b2", ACT.Tanh, "z2", p, 0)
             scalar("a0", ACT.Sigmoid, "s0", p, 0)
-            vector("p3", "m3", ALU.mult, "c3", p, 0)
             vector_relu("z0", "s1", ALU.mult, "a0", p, 0)
+            vector("p3", "m3", ALU.mult, "c3", p, 0)
             scalar("b3", ACT.Sigmoid, "z3", p, 0)
             scalar("a2", ACT.Sigmoid, "s2", p, 0)
             scalar("new_m", ACT.Tanh, "z6", p, 2)

@@ -48,8 +48,6 @@ def tile_nascell_kernel(tc, x, m_prev, c_prev, w_m_words, w_m_scales, w_inputs_w
         s_sb = (s_x, s_m)
 
         nc.gpsimd.memset(heat[:], 0.0)
-        nc.vector.memset(s_x[:].bitcast(I32), 0)
-        nc.vector.memset(s_m[:].bitcast(I32), 0)
         nc.vector.memset(warm[:], 0.0)
         nc.scalar.activation(out=warm[:], in_=warm[:], func=ACT.Sigmoid)
         make_identity(nc, ident[:])
@@ -65,11 +63,11 @@ def tile_nascell_kernel(tc, x, m_prev, c_prev, w_m_words, w_m_scales, w_inputs_w
             for r in range(4):
                 nc.sync.dma_start(out=s_sb[o][r:P:32, :].bitcast(I32), in_=scales_d[o][r:16:4, :].bitcast(I32))
 
+        load_scales(0)
         load_rows(0, 0, 1)
         load_rows(1, 0, 1)
         load_words(0, 4, 4)
         load_words(1, 4, 4)
-        load_scales(0)
         load_scales(1)
         load_words(0, 5, 5)
         load_words(1, 5, 5)

@@ -63,14 +63,12 @@ def tile_nascell_kernel(tc, x, m_prev, c_prev, w_m_words, w_m_scales, w_inputs_w
             for r in range(4):
                 nc.sync.dma_start(out=s_sb[o][r:P:32, :].bitcast(I32), in_=scales_d[o][r:16:4, :].bitcast(I32))
 
-        load_scales(0)
         load_rows(0, 0, 1)
+        load_scales(0)
         load_rows(1, 0, 1)
-        load_words(0, 4, 4)
-        load_words(1, 4, 4)
+        load_words(0, 4, 5)
+        load_words(1, 4, 5)
         load_scales(1)
-        load_words(0, 5, 5)
-        load_words(1, 5, 5)
         load_words(0, 6, 7)
         load_words(1, 6, 7)
         load_rows(0, 1, 2)
@@ -198,11 +196,11 @@ def tile_nascell_kernel(tc, x, m_prev, c_prev, w_m_words, w_m_scales, w_inputs_w
             product("x3", p, 3, (0,))
             product("m3", p, 3, (1,))
 
-            vector("z5", "b2", ALU.add, "b3", p, 1)
             vector_relu("z1", "p3", ALU.add, "a2", p, 1)
             scalar("a4", ACT.Tanh, "s4", p, 0)
             scalar("u0", ACT.Tanh, "z0", p, 1)
             vector("v0", "u0", ALU.add, "c", p, 1)
+            vector("z5", "b2", ALU.add, "b3", p, 1)
             scalar("a5", ACT.Sigmoid, "s5", p, 0)
             vector("z2", "a4", ALU.mult, "a5", p, 0)
             scalar("b1", ACT.Tanh, "z1", p, 1)
@@ -218,11 +216,14 @@ def tile_nascell_kernel(tc, x, m_prev, c_prev, w_m_words, w_m_scales, w_inputs_w
             if p == 0:
                 quantise(p + 1, 0, 2)
             scalar("l3", ACT.Tanh, "z5", p, 1)
-            vector_copy("c3", "x3", p, 0)
+            if p > 0:
+                vector_copy("c3", "x3", p, 0)
             vector("z6", "new_c", ALU.mult, "l3", p, 1)
             scalar("b2", ACT.Tanh, "z2", p, 0)
             scalar("a0", ACT.Sigmoid, "s0", p, 0)
             vector_relu("z0", "s1", ALU.mult, "a0", p, 0)
+            if p == 0:
+                vector_copy("c3", "x3", p, 0)
             vector("p3", "m3", ALU.mult, "c3", p, 0)
             scalar("b3", ACT.Sigmoid, "z3", p, 0)
             scalar("a2", ACT.Sigmoid, "s2", p, 0)

@@ -63,12 +63,14 @@ def tile_nascell_kernel(tc, x, m_prev, c_prev, w_m_words, w_m_scales, w_inputs_w
             for r in range(4):
                 nc.sync.dma_start(out=s_sb[o][r:P:32, :].bitcast(I32), in_=scales_d[o][r:16:4, :].bitcast(I32))
 
-        load_rows(0, 0, 1)
         load_scales(0)
+        load_rows(0, 0, 1)
         load_rows(1, 0, 1)
-        load_words(0, 4, 5)
-        load_words(1, 4, 5)
+        load_words(0, 4, 4)
+        load_words(1, 4, 4)
         load_scales(1)
+        load_words(0, 5, 5)
+        load_words(1, 5, 5)
         load_words(0, 6, 7)
         load_words(1, 6, 7)
         load_rows(0, 1, 2)

@@ -21,6 +21,83 @@ FLOPS = 2 * 2 * B * K * GATES * H
 WHOLE = (slice(0, H),)
 HALVES = (slice(0, H // 2), slice(H // 2, H))
 
+FIRST = (
+    ("a4", 0),
+    ("a5", 0),
+    ("z2", 0),
+    ("regroup", -1),
+    ("a6", 0),
+    ("a7", 0),
+    ("z3", 0),
+    ("quantise", -1),
+    ("C", 0),
+    ("a0", 0),
+    ("z0", 0),
+    ("c3", 0),
+    ("p3", 0),
+    ("b3", 0),
+    ("a2", 0),
+)
+SECOND = (
+    ("z1", 1),
+    ("a4", 0),
+    ("u0", 1),
+    ("v0", 1),
+    ("z5", 1),
+    ("a5", 0),
+    ("z2", 0),
+    ("b1", 1),
+    ("regroup", -1),
+    ("b0", 1),
+    ("new_c", 1),
+    ("store_c", 1),
+    ("quantise", -1),
+    ("a6", 0),
+    ("a7", 0),
+    ("z3", 0),
+    ("c3", 0),
+    ("C", 0),
+    ("z6", 1),
+    ("a0", 0),
+    ("z0", 0),
+    ("p3", 0),
+    ("b3", 0),
+    ("a2", 0),
+    ("new_m", 2),
+    ("store_m", 2),
+)
+PAIRED = {
+    "z6": ("end_in", 2, 0), "z0": ("end_in", 1, 1), "new_m": ("end_out", 2, 0), "u0": ("end_out", 1, 1),
+    "z1": ("mid_in", 1, 0), "v0": ("mid_in", 1, 1), "b1": ("mid_out", 1, 0), "b0": ("mid_out", 1, 1),
+    "z5": ("low_in", 1, 0), "z2": ("low_in", 0, 1), "l3": ("low_out", 1, 0), "b2": ("low_out", 0, 1),
+}
+STEADY = (
+    ("z1", 1),
+    ("A", 0),
+    ("store_m", 2),
+    ("v0", 1),
+    ("z5", 1),
+    ("a4", 0),
+    ("a5", 0),
+    ("z2", 0),
+    ("regroup", -1),
+    ("B", 0),
+    ("new_c", 1),
+    ("store_c", 1),
+    ("quantise", -1),
+    ("a6", 0),
+    ("a7", 0),
+    ("z3", 0),
+    ("c3", 0),
+    ("C", 0),
+    ("z6", 1),
+    ("a0", 0),
+    ("z0", 0),
+    ("p3", 0),
+    ("b3", 0),
+    ("a2", 0),
+)
+
 
 def tile_nascell_kernel(tc, x, m_prev, c_prev, w_m_words, w_m_scales, w_inputs_words, w_inputs_scales, out_0, out_1):
     nc = tc.nc
@@ -41,19 +118,22 @@ def tile_nascell_kernel(tc, x, m_prev, c_prev, w_m_words, w_m_scales, w_inputs_w
         w_m = keep.tile([P, 2 * GATES * H], U8, align_bytes=64)
         s_x = keep.tile([P, GATES * H], U8, align_bytes=64)
         s_m = keep.tile([P, GATES * H], U8, align_bytes=64)
+        s_sb = (s_x, s_m)
         grouped = keep.tile([P, TILES, 2, 4 * P], BF16, align_bytes=64)
         codes = keep.tile([P, TILES, 2, P], U32, align_bytes=64)
         a_scales = keep.tile([P, TILES, 2, P], U8, align_bytes=64)
         w_sb = (w_x, w_m)
-        s_sb = (s_x, s_m)
 
         nc.gpsimd.memset(heat[:], 0.0)
         nc.vector.memset(warm[:], 0.0)
         nc.scalar.activation(out=warm[:], in_=warm[:], func=ACT.Sigmoid)
         make_identity(nc, ident[:])
 
-        def load_rows(o, lo, hi):
-            nc.sync.dma_start(out=act_sb[:, o, lo:hi, :], in_=act_d[o][:, lo:hi, :])
+        def load_rows(o, lo, hi, queue=nc.sync):
+            queue.dma_start(out=act_sb[:, o, lo:hi, :], in_=act_d[o][:, lo:hi, :])
+
+        def load_c(lo, hi, queue=nc.sync):
+            queue.dma_start(out=c_sb[:, lo:hi, :], in_=c_v[:, lo:hi, :])
 
         def load_words(o, first, last):
             cols = slice(first * 2 * H, (last + 1) * 2 * H)
@@ -79,20 +159,17 @@ def tile_nascell_kernel(tc, x, m_prev, c_prev, w_m_words, w_m_scales, w_inputs_w
         load_words(1, 0, 1)
         load_words(0, 2, 3)
         load_words(1, 2, 3)
-        nc.sync.dma_start(out=c_sb[:, 0:2, :], in_=c_v[:, 0:2, :])
+        load_c(0, 2)
         load_rows(0, 2, 4)
         load_rows(1, 2, 4)
         load_rows(0, 4, 8)
         load_rows(1, 4, 8)
-        nc.sync.dma_start(out=c_sb[:, 2:TILES, :], in_=c_v[:, 2:TILES, :])
+        load_c(2, TILES)
 
         live = {}
 
         def there(i):
             return 0 <= i < TILES
-
-        def cuts(p):
-            return WHOLE if p < TILES else HALVES
 
         def flip(i, lo, hi):
             if there(i):
@@ -133,42 +210,99 @@ def tile_nascell_kernel(tc, x, m_prev, c_prev, w_m_words, w_m_scales, w_inputs_w
                     )
                 live[(name, i)] = bank[:]
 
+        pairs = {}
+
         def fresh(name, i):
-            made = work.tile([P, H], F32, tag=name, name=name)
-            live[(name, i)] = made[:]
-            return made[:]
+            if name in PAIRED:
+                tag, ahead, member = PAIRED[name]
+                if (tag, i + ahead) not in pairs:
+                    pair = work.tile([P, 2, H], F32, tag=tag, name=tag)
+                    pairs[(tag, i + ahead)] = pair
+                made = pairs[(tag, i + ahead)][:, member, :]
+            else:
+                single = work.tile([P, H], F32, tag=name, name=name)
+                made = single[:]
+            live[(name, i)] = made
+            return made
 
-        def scalar(name, func, src, p, lag):
-            i = p - lag
-            if there(i):
+        def scalar_pair(first, second, src):
+            def run(p, cuts):
+                tag = PAIRED[first][0]
+                i, j = p - PAIRED[first][1], p - PAIRED[second][1]
+                if there(i) and there(j) and p < TILES:
+                    fresh(first, i)
+                    fresh(second, j)
+                    nc.scalar.activation(out=pairs[(tag, p)][:].rearrange("p m h -> p (m h)"), in_=pairs[(PAIRED[src][0], p)][:].rearrange("p m h -> p (m h)"), func=ACT.Tanh)
+                else:
+                    for name, n in ((first, i), (second, j)):
+                        if there(n):
+                            stages[name](n, cuts)
+            return run
+
+        def scalar(name, func, src):
+            def run(i, cuts):
                 out = fresh(name, i)
-                for cols in cuts(p):
+                for cols in cuts:
                     nc.scalar.activation(out=out[:, cols], in_=live[(src, i)][:, cols], func=func)
+            return run
 
-        def vector(name, a, op, b, p, lag):
-            i = p - lag
-            if there(i):
+        def vector(name, a, op, b):
+            def run(i, cuts):
                 out = fresh(name, i)
-                for cols in cuts(p):
+                for cols in cuts:
                     nc.vector.tensor_tensor(out=out[:, cols], in0=live[(a, i)][:, cols], in1=live[(b, i)][:, cols], op=op)
+            return run
 
-        def vector_relu(name, a, op, b, p, lag):
-            i = p - lag
-            if there(i):
+        def vector_relu(name, a, op, b):
+            def run(i, cuts):
                 out = fresh(name, i)
-                for cols in cuts(p):
+                for cols in cuts:
                     nc.vector.scalar_tensor_tensor(out=out[:, cols], in0=live[(a, i)][:, cols], scalar=0.0, in1=live[(b, i)][:, cols], op0=ALU.max, op1=op)
+            return run
 
-        def vector_copy(name, a, p, lag):
-            i = p - lag
-            if there(i):
+        def vector_copy(name, a):
+            def run(i, cuts):
                 nc.vector.tensor_copy(out=fresh(name, i), in_=live[(a, i)])
+            return run
 
-        def store(dram, name, p, lag):
-            i = p - lag
-            if there(i):
-                for cols in cuts(p):
+        def store(dram, name):
+            def run(i, cuts):
+                for cols in cuts:
                     nc.sync.dma_start(out=dram[:, i, cols], in_=live[(name, i)][:, cols])
+            return run
+
+        stages = {
+            "a0": scalar("a0", ACT.Sigmoid, "s0"),
+            "a2": scalar("a2", ACT.Sigmoid, "s2"),
+            "a4": scalar("a4", ACT.Tanh, "s4"),
+            "a5": scalar("a5", ACT.Sigmoid, "s5"),
+            "a6": scalar("a6", ACT.Tanh, "s6"),
+            "a7": scalar("a7", ACT.Sigmoid, "s7"),
+            "u0": scalar("u0", ACT.Tanh, "z0"),
+            "b0": scalar("b0", ACT.Tanh, "v0"),
+            "b1": scalar("b1", ACT.Tanh, "z1"),
+            "b2": scalar("b2", ACT.Tanh, "z2"),
+            "b3": scalar("b3", ACT.Sigmoid, "z3"),
+            "l3": scalar("l3", ACT.Tanh, "z5"),
+            "new_m": scalar("new_m", ACT.Tanh, "z6"),
+            "c3": vector_copy("c3", "x3"),
+            "p3": vector("p3", "m3", ALU.mult, "c3"),
+            "z0": vector_relu("z0", "s1", ALU.mult, "a0"),
+            "z1": vector_relu("z1", "p3", ALU.add, "a2"),
+            "z2": vector("z2", "a4", ALU.mult, "a5"),
+            "z3": vector("z3", "a6", ALU.add, "a7"),
+            "z5": vector("z5", "b2", ALU.add, "b3"),
+            "z6": vector("z6", "new_c", ALU.mult, "l3"),
+            "v0": vector("v0", "u0", ALU.add, "c"),
+            "new_c": vector("new_c", "b0", ALU.mult, "b1"),
+            "regroup": lambda i, cuts: regroup(i, 0, 2),
+            "quantise": lambda i, cuts: quantise(i, 0, 2),
+            "A": scalar_pair("new_m", "u0", "z6"),
+            "B": scalar_pair("b1", "b0", "z1"),
+            "C": scalar_pair("l3", "b2", "z5"),
+            "store_c": store(new_c_v, "new_c"),
+            "store_m": store(new_m_v, "new_m"),
+        }
 
         for i in range(TILES):
             live[("c", i)] = c_sb[:, i, :]
@@ -177,6 +311,17 @@ def tile_nascell_kernel(tc, x, m_prev, c_prev, w_m_words, w_m_scales, w_inputs_w
             unread = psum.tile([P, H], F32, tag="bank", name="unread")
             for n in range(count):
                 nc.tensor.matmul(out=unread[:], lhsT=heat[:, 0:P], rhs=heat[:], start=True, stop=True)
+
+        def upper_gates(i):
+            for g in (4, 5, 6, 7):
+                product("s%d" % g, i, g, (0, 1))
+
+        def lower_gates(i):
+            product("s0", i, 0, (0, 1))
+            product("s1", i, 1, (0, 1))
+            product("s2", i, 2, (0, 1))
+            product("x3", i, 3, (0,))
+            product("m3", i, 3, (1,))
 
         heat_tensor(5)
         flip(0, 0, 1)
@@ -187,47 +332,10 @@ def tile_nascell_kernel(tc, x, m_prev, c_prev, w_m_words, w_m_scales, w_inputs_w
         quantise(0, 0, 1)
         quantise(0, 1, 2)
         for p in range(TILES + 2):
-            product("s4", p, 4, (0, 1))
-            product("s5", p, 5, (0, 1))
-            product("s6", p, 6, (0, 1))
-            product("s7", p, 7, (0, 1))
+            cuts = WHOLE if p < TILES else HALVES
+            upper_gates(p)
             flip(p + 1, 0, 2)
-            product("s0", p, 0, (0, 1))
-            product("s1", p, 1, (0, 1))
-            product("s2", p, 2, (0, 1))
-            product("x3", p, 3, (0,))
-            product("m3", p, 3, (1,))
-
-            vector_relu("z1", "p3", ALU.add, "a2", p, 1)
-            scalar("a4", ACT.Tanh, "s4", p, 0)
-            scalar("u0", ACT.Tanh, "z0", p, 1)
-            vector("v0", "u0", ALU.add, "c", p, 1)
-            vector("z5", "b2", ALU.add, "b3", p, 1)
-            scalar("a5", ACT.Sigmoid, "s5", p, 0)
-            vector("z2", "a4", ALU.mult, "a5", p, 0)
-            scalar("b1", ACT.Tanh, "z1", p, 1)
-            regroup(p + 1, 0, 2)
-            scalar("b0", ACT.Tanh, "v0", p, 1)
-            vector("new_c", "b0", ALU.mult, "b1", p, 1)
-            store(new_c_v, "new_c", p, 1)
-            if p > 0:
-                quantise(p + 1, 0, 2)
-            scalar("a6", ACT.Tanh, "s6", p, 0)
-            scalar("a7", ACT.Sigmoid, "s7", p, 0)
-            vector("z3", "a6", ALU.add, "a7", p, 0)
-            if p == 0:
-                quantise(p + 1, 0, 2)
-            scalar("l3", ACT.Tanh, "z5", p, 1)
-            if p > 0:
-                vector_copy("c3", "x3", p, 0)
-            vector("z6", "new_c", ALU.mult, "l3", p, 1)
-            scalar("b2", ACT.Tanh, "z2", p, 0)
-            scalar("a0", ACT.Sigmoid, "s0", p, 0)
-            vector_relu("z0", "s1", ALU.mult, "a0", p, 0)
-            if p == 0:
-                vector_copy("c3", "x3", p, 0)
-            vector("p3", "m3", ALU.mult, "c3", p, 0)
-            scalar("b3", ACT.Sigmoid, "z3", p, 0)
-            scalar("a2", ACT.Sigmoid, "s2", p, 0)
-            scalar("new_m", ACT.Tanh, "z6", p, 2)
-            store(new_m_v, "new_m", p, 2)
+            lower_gates(p)
+            for name, lag in FIRST if p == 0 else STEADY if 3 <= p < TILES - 1 else SECOND:
+                if name in ("A", "B", "C") or there(p - lag):
+                    stages[name](p - lag, cuts)

import concourse.mybir as mybir
from concourse.masks import make_identity

F32 = mybir.dt.float32
BF16 = mybir.dt.bfloat16
I32 = mybir.dt.int32
U8 = mybir.dt.uint8
U32 = mybir.dt.uint32
FP8X4 = mybir.dt.float8_e4m3fn_x4
FP4X4 = mybir.dt.float4_e2m1fn_x4
ACT = mybir.ActivationFunctionType
ALU = mybir.AluOpType

P = 128
B = 1024
K = 512
H = 512
GATES = 8
TILES = B // P
FLOPS = 2 * 2 * B * K * GATES * H
WHOLE = (slice(0, H),)
HALVES = (slice(0, H // 2), slice(H // 2, H))

FIRST = (
    ("a4", 0),
    ("a5", 0),
    ("z2", 0),
    ("regroup", -1),
    ("a6", 0),
    ("a7", 0),
    ("z3", 0),
    ("quantise", -1),
    ("C", 0),
    ("a0", 0),
    ("z0", 0),
    ("c3", 0),
    ("p3", 0),
    ("b3", 0),
    ("a2", 0),
)
SECOND = (
    ("z1", 1),
    ("a4", 0),
    ("u0", 1),
    ("v0", 1),
    ("z5", 1),
    ("a5", 0),
    ("z2", 0),
    ("b1", 1),
    ("regroup", -1),
    ("b0", 1),
    ("new_c", 1),
    ("store_c", 1),
    ("quantise", -1),
    ("a6", 0),
    ("a7", 0),
    ("z3", 0),
    ("c3", 0),
    ("C", 0),
    ("z6", 1),
    ("a0", 0),
    ("z0", 0),
    ("p3", 0),
    ("b3", 0),
    ("a2", 0),
    ("new_m", 2),
    ("store_m", 2),
)
PAIRED = {
    "z6": ("end_in", 2, 0), "z0": ("end_in", 1, 1), "new_m": ("end_out", 2, 0), "u0": ("end_out", 1, 1),
    "z1": ("mid_in", 1, 0), "v0": ("mid_in", 1, 1), "b1": ("mid_out", 1, 0), "b0": ("mid_out", 1, 1),
    "z5": ("low_in", 1, 0), "z2": ("low_in", 0, 1), "l3": ("low_out", 1, 0), "b2": ("low_out", 0, 1),
}
STEADY = (
    ("z1", 1),
    ("A", 0),
    ("store_m", 2),
    ("v0", 1),
    ("z5", 1),
    ("a4", 0),
    ("a5", 0),
    ("z2", 0),
    ("regroup", -1),
    ("B", 0),
    ("new_c", 1),
    ("store_c", 1),
    ("quantise", -1),
    ("a6", 0),
    ("a7", 0),
    ("z3", 0),
    ("c3", 0),
    ("C", 0),
    ("z6", 1),
    ("a0", 0),
    ("z0", 0),
    ("p3", 0),
    ("b3", 0),
    ("a2", 0),
)


def tile_nascell_kernel(tc, x, m_prev, c_prev, w_m_words, w_m_scales, w_inputs_words, w_inputs_scales, out_0, out_1):
    nc = tc.nc
    act_d = (x.rearrange("(p i) k -> p i k", i=TILES), m_prev.rearrange("(p i) k -> p i k", i=TILES))
    c_v = c_prev.rearrange("(p i) k -> p i k", i=TILES)
    new_m_v = out_0.rearrange("(p i) h -> p i h", i=TILES)
    new_c_v = out_1.rearrange("(p i) h -> p i h", i=TILES)
    words_d = (w_inputs_words.flatten_outer_dims(), w_m_words.flatten_outer_dims())
    scales_d = (w_inputs_scales.flatten_outer_dims(), w_m_scales.flatten_outer_dims())

    with tc.tile_pool(name="keep", bufs=1) as keep, tc.tile_pool(name="work", bufs=3) as work, tc.psum_pool(name="psum", bufs=8) as psum, tc.manual_schedule():
        ident = keep.tile([P, P], F32)
        warm = keep.tile([P, 1], F32)
        heat = keep.tile([P, H], BF16)
        act_sb = keep.tile([P, 2, TILES, K], BF16)
        c_sb = keep.tile([P, TILES, H], BF16)
        w_x = keep.tile([P, 2 * GATES * H], U8, align_bytes=64)
        w_m = keep.tile([P, 2 * GATES * H], U8, align_bytes=64)
        s_x = keep.tile([P, GATES * H], U8, align_bytes=64)
        s_m = keep.tile([P, GATES * H], U8, align_bytes=64)
        s_sb = (s_x, s_m)
        grouped = keep.tile([P, TILES, 2, 4 * P], BF16, align_bytes=64)
        codes = keep.tile([P, TILES, 2, P], U32, align_bytes=64)
        a_scales = keep.tile([P, TILES, 2, P], U8, align_bytes=64)
        w_sb = (w_x, w_m)

        nc.gpsimd.memset(heat[:], 0.0)
        nc.vector.memset(warm[:], 0.0)
        nc.scalar.activation(out=warm[:], in_=warm[:], func=ACT.Sigmoid)
        make_identity(nc, ident[:])

        def load_rows(o, lo, hi, queue=nc.sync):
            queue.dma_start(out=act_sb[:, o, lo:hi, :], in_=act_d[o][:, lo:hi, :])

        def load_c(lo, hi, queue=nc.sync):
            queue.dma_start(out=c_sb[:, lo:hi, :], in_=c_v[:, lo:hi, :])

        def load_words(o, first, last):
            cols = slice(first * 2 * H, (last + 1) * 2 * H)
            nc.sync.dma_start(out=w_sb[o][:, cols].bitcast(I32), in_=words_d[o][:, cols].bitcast(I32))

        def load_scales(o):
            for r in range(4):
                nc.sync.dma_start(out=s_sb[o][r:P:32, :].bitcast(I32), in_=scales_d[o][r:16:4, :].bitcast(I32))

        load_scales(0)
        load_rows(0, 0, 1)
        load_rows(1, 0, 1)
        load_words(0, 4, 4)
        load_words(1, 4, 4)
        load_scales(1)
        load_words(0, 5, 5)
        load_words(1, 5, 5)
        load_words(0, 6, 7)
        load_words(1, 6, 7)
        load_rows(0, 1, 2)
        load_rows(1, 1, 2)
        load_words(0, 0, 1)
        load_words(1, 0, 1)
        load_words(0, 2, 3)
        load_words(1, 2, 3)
        load_c(0, 2)
        load_rows(0, 2, 4)
        load_rows(1, 2, 4)
        load_rows(0, 4, 8)
        load_rows(1, 4, 8)
        load_c(2, TILES)

        live = {}

        def there(i):
            return 0 <= i < TILES

        def flip(i, lo, hi):
            if there(i):
                flipped = psum.tile([P, hi - lo, 2, P], F32, tag="bank")
                for o in range(lo, hi):
                    as_words = act_sb[:, o, i, :].bitcast(F32)
                    for u in range(2):
                        nc.tensor.transpose(flipped[:, o - lo, u, :], as_words[:, u:K // 2:2], ident[:])
                live[("flipped", i, lo)] = flipped

        def regroup(i, lo, hi):
            if there(i):
                nc.vector.tensor_copy(
                    out=grouped[:, i, lo:hi].bitcast(F32).rearrange("p o (r u) -> p o r u", u=2),
                    in_=live[("flipped", i, lo)][:].rearrange("p o u r -> p o r u"),
                )

        def quantise(i, lo, hi):
            if there(i):
                nc.vector.quantize_mx(
                    out=codes[:, i, lo:hi].rearrange("p o r -> p (o r)").bitcast(FP8X4),
                    scales=a_scales[:, i, lo:hi].rearrange("p o r -> p (o r)"),
                    in_=grouped[:, i, lo:hi].rearrange("p o c -> p (o c)"),
                )

        def product(name, i, g, operands):
            if there(i):
                bank = psum.tile([P, H], F32, tag="bank", name=name)
                for o in operands:
                    nc.tensor.matmul_mx(
                        out=bank[:],
                        lhsT=codes[:, i, o, :].bitcast(FP8X4),
                        lhsT_scale=a_scales[:, i, o, :],
                        rhs=w_sb[o][:, g * 2 * H:(g + 1) * 2 * H].bitcast(FP4X4),
                        rhs_scale=s_sb[o][:, g * H:(g + 1) * H],
                        start=(o == operands[0]),
                        stop=(o == operands[-1]),
                    )
                live[(name, i)] = bank[:]

        pairs = {}

        def fresh(name, i):
            if name in PAIRED:
                tag, ahead, member = PAIRED[name]
                if (tag, i + ahead) not in pairs:
                    pair = work.tile([P, 2, H], F32, tag=tag, name=tag)
                    pairs[(tag, i + ahead)] = pair
                made = pairs[(tag, i + ahead)][:, member, :]
            else:
                single = work.tile([P, H], F32, tag=name, name=name)
                made = single[:]
            live[(name, i)] = made
            return made

        def scalar_pair(first, second, src):
            def run(p, cuts):
                tag = PAIRED[first][0]
                i, j = p - PAIRED[first][1], p - PAIRED[second][1]
                if there(i) and there(j) and p < TILES:
                    fresh(first, i)
                    fresh(second, j)
                    nc.scalar.activation(out=pairs[(tag, p)][:].rearrange("p m h -> p (m h)"), in_=pairs[(PAIRED[src][0], p)][:].rearrange("p m h -> p (m h)"), func=ACT.Tanh)
                else:
                    for name, n in ((first, i), (second, j)):
                        if there(n):
                            stages[name](n, cuts)
            return run

        def scalar(name, func, src):
            def run(i, cuts):
                out = fresh(name, i)
                for cols in cuts:
                    nc.scalar.activation(out=out[:, cols], in_=live[(src, i)][:, cols], func=func)
            return run

        def vector(name, a, op, b):
            def run(i, cuts):
                out = fresh(name, i)
                for cols in cuts:
                    nc.vector.tensor_tensor(out=out[:, cols], in0=live[(a, i)][:, cols], in1=live[(b, i)][:, cols], op=op)
            return run

        def vector_relu(name, a, op, b):
            def run(i, cuts):
                out = fresh(name, i)
                for cols in cuts:
                    nc.vector.scalar_tensor_tensor(out=out[:, cols], in0=live[(a, i)][:, cols], scalar=0.0, in1=live[(b, i)][:, cols], op0=ALU.max, op1=op)
            return run

        def vector_copy(name, a):
            def run(i, cuts):
                nc.vector.tensor_copy(out=fresh(name, i), in_=live[(a, i)])
            return run

        def store(dram, name):
            def run(i, cuts):
                for cols in cuts:
                    nc.sync.dma_start(out=dram[:, i, cols], in_=live[(name, i)][:, cols])
            return run

        stages = {
            "a0": scalar("a0", ACT.Sigmoid, "s0"),
            "a2": scalar("a2", ACT.Sigmoid, "s2"),
            "a4": scalar("a4", ACT.Tanh, "s4"),
            "a5": scalar("a5", ACT.Sigmoid, "s5"),
            "a6": scalar("a6", ACT.Tanh, "s6"),
            "a7": scalar("a7", ACT.Sigmoid, "s7"),
            "u0": scalar("u0", ACT.Tanh, "z0"),
            "b0": scalar("b0", ACT.Tanh, "v0"),
            "b1": scalar("b1", ACT.Tanh, "z1"),
            "b2": scalar("b2", ACT.Tanh, "z2"),
            "b3": scalar("b3", ACT.Sigmoid, "z3"),
            "l3": scalar("l3", ACT.Tanh, "z5"),
            "new_m": scalar("new_m", ACT.Tanh, "z6"),
            "c3": vector_copy("c3", "x3"),
            "p3": vector("p3", "m3", ALU.mult, "c3"),
            "z0": vector_relu("z0", "s1", ALU.mult, "a0"),
            "z1": vector_relu("z1", "p3", ALU.add, "a2"),
            "z2": vector("z2", "a4", ALU.mult, "a5"),
            "z3": vector("z3", "a6", ALU.add, "a7"),
            "z5": vector("z5", "b2", ALU.add, "b3"),
            "z6": vector("z6", "new_c", ALU.mult, "l3"),
            "v0": vector("v0", "u0", ALU.add, "c"),
            "new_c": vector("new_c", "b0", ALU.mult, "b1"),
            "regroup": lambda i, cuts: regroup(i, 0, 2),
            "quantise": lambda i, cuts: quantise(i, 0, 2),
            "A": scalar_pair("new_m", "u0", "z6"),
            "B": scalar_pair("b1", "b0", "z1"),
            "C": scalar_pair("l3", "b2", "z5"),
            "store_c": store(new_c_v, "new_c"),
            "store_m": store(new_m_v, "new_m"),
        }

        for i in range(TILES):
            live[("c", i)] = c_sb[:, i, :]

        def heat_tensor(count):
            unread = psum.tile([P, H], F32, tag="bank", name="unread")
            for n in range(count):
                nc.tensor.matmul(out=unread[:], lhsT=heat[:, 0:P], rhs=heat[:], start=True, stop=True)

        def upper_gates(i):
            for g in (4, 5, 6, 7):
                product("s%d" % g, i, g, (0, 1))

        def lower_gates(i):
            product("s0", i, 0, (0, 1))
            product("s1", i, 1, (0, 1))
            product("s2", i, 2, (0, 1))
            product("x3", i, 3, (0,))
            product("m3", i, 3, (1,))

        heat_tensor(5)
        flip(0, 0, 1)
        flip(0, 1, 2)
        heat_tensor(2)
        regroup(0, 0, 1)
        regroup(0, 1, 2)
        quantise(0, 0, 1)
        quantise(0, 1, 2)
        for p in range(TILES + 2):
            cuts = WHOLE if p < TILES else HALVES
            upper_gates(p)
            flip(p + 1, 0, 2)
            lower_gates(p)
            for name, lag in FIRST if p == 0 else STEADY if 3 <= p < TILES - 1 else SECOND:
                if name in ("A", "B", "C") or there(p - lag):
                    stages[name](p - lag, cuts)
